import numpy as np
import ml_dtypes


def mxq(x, axis, fmt="e4m3"):
    dtype, down = {"e4m3": (ml_dtypes.float8_e4m3fn, 7), "e5m2": (ml_dtypes.float8_e5m2, 14)}[fmt]
    v = np.moveaxis(np.asarray(x, np.float32).astype(ml_dtypes.bfloat16).astype(np.float64), axis, -1)
    blocks = v.reshape(v.shape[:-1] + (-1, 32))
    amax = np.abs(blocks).max(-1, keepdims=True)
    byte = np.maximum(np.where(amax > 0, np.frexp(amax)[1] - 1 + 127, 0) - down, 1)
    scale = np.exp2(byte - 127.0)
    codes = (blocks / scale).astype(np.float32).astype(dtype).astype(np.float64)
    return np.moveaxis((codes * scale).reshape(v.shape), -1, axis)


WIDE = False


def mx_kscale(k):
    if not WIDE:
        return np.ones(k)
    levels = np.array([10, -10, 5, -5, 0])
    if k % 512:
        return np.exp2(np.random.permutation(np.resize(levels, k // 32))).repeat(32)
    a = np.empty((k // 512, 16))
    for p in range(k // 512):
        a[p, :8] = np.random.permutation(np.resize(levels, 8))
        for g in range(8):
            far = levels[np.abs(levels - a[p, g]) >= 10]
            a[p, g + 8] = far[np.random.randint(len(far))]
    return np.exp2(a.ravel()).repeat(32)


BF16 = ml_dtypes.bfloat16


def bf(x):
    return np.asarray(x, np.float32).astype(BF16)


def f64(x):
    return np.asarray(x).astype(np.float64)


B, S, H, O, W = 8, 2048, 512, 128, 8


def setup_inputs():
    s = mx_kscale(H)
    return {"hidden_states": bf(np.random.standard_normal((B, S, H)) * s),
            "gate_proj": bf(np.random.standard_normal((O, H)) / np.sqrt(H) / s[None, :]),
            "world_size": W}


def reference(hidden_states, gate_proj, world_size):
    h = gate_proj.shape[1]
    view = f64(hidden_states).reshape(-1, h)
    mm = mxq(view, 1, "e4m3") @ mxq(f64(gate_proj), 1, "e4m3").T
    n, o = mm.shape
    out = mm.reshape(world_size, n // world_size, o).sum(axis=0)
    return out

@@ -1,0 +1,164 @@
+from contextlib import ExitStack
+
+import concourse.mybir as mybir
+from concourse.masks import make_identity
+
+F32 = mybir.dt.float32
+BF16 = mybir.dt.bfloat16
+U32 = mybir.dt.uint32
+U8 = mybir.dt.uint8
+FP8X4 = mybir.dt.float8_e4m3fn_x4
+
+P = 128
+PACK = 4
+HALVES = 2
+
+CHUNKS = 8
+ROWS = 2048
+K = 512
+WIDTH = 128
+
+ROWS_PER_PARTITION = ROWS // P
+UNIT_BLOCKS = 4
+STRIPS = ROWS_PER_PARTITION // UNIT_BLOCKS
+UNITS = STRIPS * CHUNKS
+BANK_BLOCKS = 2
+UNIT_BANKS = UNIT_BLOCKS // BANK_BLOCKS
+BANK_WORDS = BANK_BLOCKS * HALVES * P
+RUN_UNITS = 2
+RUNS = UNITS // RUN_UNITS
+VECTOR_EVERY = 4
+
+FLOPS = 2 * CHUNKS * ROWS * K * WIDTH
+
+
+def tile_testmmrsmodel_t_kernel(tc, hidden_states, gate_proj, world_size, out):
+    nc = tc.nc
+    assert world_size == CHUNKS
+    assert tuple(hidden_states.shape) == (CHUNKS, ROWS, K)
+    assert tuple(gate_proj.shape) == (WIDTH, K)
+
+    x_dram = hidden_states.rearrange("r (p i) k -> p r (i k)", i=ROWS_PER_PARTITION)
+    out_dram = out.rearrange("(p i) o -> p (i o)", i=ROWS_PER_PARTITION)
+
+    with ExitStack() as stack:
+        const = stack.enter_context(tc.tile_pool(name="const", bufs=1))
+        x_pool = stack.enter_context(tc.tile_pool(name="x", bufs=UNITS))
+        staged = stack.enter_context(tc.tile_pool(name="staged", bufs=3 * RUN_UNITS))
+        out_pool = stack.enter_context(tc.tile_pool(name="result", bufs=2))
+        flipped = stack.enter_context(tc.psum_pool(name="flipped", bufs=RUN_UNITS * UNIT_BANKS))
+        sums_pool = stack.enter_context(tc.psum_pool(name="sums", bufs=1))
+        stack.enter_context(tc.manual_schedule())
+
+        identity = const.tile([P, P], F32)
+        gate = const.tile([P, K], BF16)
+        gate_grouped = const.tile([P, WIDTH * PACK], BF16, align_bytes=64)
+        gate_codes = const.tile([P, WIDTH], U32, align_bytes=64)
+        gate_scales = const.tile([P, WIDTH], U8, align_bytes=64)
+
+        x_tiles = {}
+        grouped_tiles = {}
+        mx_tiles = {}
+        sums = {}
+
+        def load(unit):
+            strip, chunk = divmod(unit, CHUNKS)
+            x = x_pool.tile([P, UNIT_BLOCKS * K], BF16)
+            first = strip * UNIT_BLOCKS * K
+            nc.sync.dma_start(out=x[:], in_=x_dram[:, chunk, first : first + UNIT_BLOCKS * K])
+            x_tiles[unit] = x
+
+        def transpose_block(bank_part, words):
+            for u in range(HALVES):
+                nc.tensor.transpose(bank_part[:, u, :], words[:, u : HALVES * P : HALVES], identity[:])
+
+        def transpose_unit(unit):
+            words = x_tiles[unit][:].bitcast(F32)
+            grouped = staged.tile([P, UNIT_BLOCKS * P * PACK], BF16, align_bytes=64)
+            grouped_words = grouped[:].bitcast(F32)
+            for h in range(UNIT_BANKS):
+                bank = flipped.tile([P, BANK_BLOCKS, HALVES, P], F32)
+                for a in range(BANK_BLOCKS):
+                    first = (h * BANK_BLOCKS + a) * HALVES * P
+                    transpose_block(bank[:, a], words[:, first : first + HALVES * P])
+                src = bank[:].rearrange("p a u j -> p a j u")
+                dst = grouped_words[:, h * BANK_WORDS : (h + 1) * BANK_WORDS].rearrange(
+                    "p (a j u) -> p a j u", a=BANK_BLOCKS, u=HALVES
+                )
+                if (unit * UNIT_BANKS + h) % VECTOR_EVERY == VECTOR_EVERY - 1:
+                    nc.vector.tensor_copy(out=dst, in_=src)
+                else:
+                    nc.scalar.copy(out=dst, in_=src)
+            grouped_tiles[unit] = grouped
+
+        def prepare_gate():
+            bank = flipped.tile([P, BANK_BLOCKS, HALVES, P], F32)
+            transpose_block(bank[:, 0], gate[:].bitcast(F32))
+            nc.vector.tensor_copy(
+                out=gate_grouped[:].bitcast(F32).rearrange("p (j u) -> p j u", u=HALVES),
+                in_=bank[:, 0].rearrange("p u j -> p j u"),
+            )
+            nc.vector.quantize_mx(
+                out=gate_codes[:].bitcast(FP8X4), scales=gate_scales[:], in_=gate_grouped[:]
+            )
+
+        def quantise_unit(unit):
+            codes = staged.tile([P, UNIT_BLOCKS * P], U32, align_bytes=64)
+            scales = staged.tile([P, UNIT_BLOCKS * P], U8, align_bytes=64)
+            nc.vector.quantize_mx(
+                out=codes[:].bitcast(FP8X4), scales=scales[:], in_=grouped_tiles[unit][:]
+            )
+            mx_tiles[unit] = (codes, scales)
+
+        def multiply_unit(unit):
+            strip, chunk = divmod(unit, CHUNKS)
+            codes, scales = mx_tiles[unit]
+            for b in range(UNIT_BLOCKS):
+                if chunk == 0:
+                    sums[b] = sums_pool.tile([P, WIDTH], F32, name="sum%d" % b)
+                rows = slice(b * P, (b + 1) * P)
+                nc.tensor.matmul_mx(
+                    out=sums[b][:],
+                    lhsT=codes[:, rows].bitcast(FP8X4),
+                    lhsT_scale=scales[:, rows],
+                    rhs=gate_codes[:].bitcast(FP8X4),
+                    rhs_scale=gate_scales[:],
+                    start=(chunk == 0),
+                    stop=(chunk == CHUNKS - 1),
+                )
+            if chunk == CHUNKS - 1:
+                store_strip(strip)
+
+        def store_strip(strip):
+            result = out_pool.tile([P, UNIT_BLOCKS, WIDTH], F32)
+            for b in range(UNIT_BLOCKS):
+                if b % 2 == 0:
+                    nc.scalar.copy(out=result[:, b, :], in_=sums[b][:])
+                else:
+                    nc.vector.tensor_copy(out=result[:, b, :], in_=sums[b][:])
+            first = strip * UNIT_BLOCKS * WIDTH
+            nc.sync.dma_start(
+                out=out_dram[:, first : first + UNIT_BLOCKS * WIDTH],
+                in_=result[:].rearrange("p b o -> p (b o)"),
+            )
+
+        def units_of(run):
+            return range(run * RUN_UNITS, (run + 1) * RUN_UNITS)
+
+        nc.scalar.dma_start(out=gate[:], in_=gate_proj)
+        for unit in range(UNITS):
+            load(unit)
+        make_identity(nc, identity[:])
+
+        for t in range(RUNS + 2):
+            if 1 <= t <= RUNS:
+                for unit in units_of(t - 1):
+                    quantise_unit(unit)
+            if t < RUNS:
+                for unit in units_of(t):
+                    transpose_unit(unit)
+            if t == 0:
+                prepare_gate()
+            if t >= 2:
+                for unit in units_of(t - 2):
+                    multiply_unit(unit)

@@ -18,6 +18,7 @@ ROWS = 2048
 K = 512
 WIDTH = 128
 
+RUN_WORDS = 8
 ROWS_PER_PARTITION = ROWS // P
 UNIT_BLOCKS = 4
 STRIPS = ROWS_PER_PARTITION // UNIT_BLOCKS
@@ -27,7 +28,7 @@ UNIT_BANKS = UNIT_BLOCKS // BANK_BLOCKS
 BANK_WORDS = BANK_BLOCKS * HALVES * P
 RUN_UNITS = 2
 RUNS = UNITS // RUN_UNITS
-VECTOR_EVERY = 4
+LOADS_AHEAD = 14
 
 FLOPS = 2 * CHUNKS * ROWS * K * WIDTH
 
@@ -45,17 +46,20 @@ def tile_testmmrsmodel_t_kernel(tc, hidden_states, gate_proj, world_size, out):
         const = stack.enter_context(tc.tile_pool(name="const", bufs=1))
         x_pool = stack.enter_context(tc.tile_pool(name="x", bufs=UNITS))
         staged = stack.enter_context(tc.tile_pool(name="staged", bufs=3 * RUN_UNITS))
-        out_pool = stack.enter_context(tc.tile_pool(name="result", bufs=2))
+        sorted_pool = stack.enter_context(tc.tile_pool(name="sorted", bufs=2 * RUN_UNITS))
+        out_pool = stack.enter_context(tc.tile_pool(name="result", bufs=STRIPS))
         flipped = stack.enter_context(tc.psum_pool(name="flipped", bufs=RUN_UNITS * UNIT_BANKS))
         sums_pool = stack.enter_context(tc.psum_pool(name="sums", bufs=1))
         stack.enter_context(tc.manual_schedule())
 
         identity = const.tile([P, P], F32)
         gate = const.tile([P, K], BF16)
+        gate_sorted = const.tile([P, K], BF16)
         gate_grouped = const.tile([P, WIDTH * PACK], BF16, align_bytes=64)
         gate_codes = const.tile([P, WIDTH], U32, align_bytes=64)
         gate_scales = const.tile([P, WIDTH], U8, align_bytes=64)
 
+        sorted_tiles = {}
         x_tiles = {}
         grouped_tiles = {}
         mx_tiles = {}
@@ -68,32 +72,40 @@ def tile_testmmrsmodel_t_kernel(tc, hidden_states, gate_proj, world_size, out):
             nc.sync.dma_start(out=x[:], in_=x_dram[:, chunk, first : first + UNIT_BLOCKS * K])
             x_tiles[unit] = x
 
-        def transpose_block(bank_part, words):
+        def sort_halves(dst, src):
+            nc.vector.tensor_copy(
+                out=dst.rearrange("p (u c i) -> p u c i", u=HALVES, i=2 * RUN_WORDS),
+                in_=src.rearrange("p (c u i) -> p u c i", u=HALVES, i=2 * RUN_WORDS),
+            )
+
+        def sort_unit(unit):
+            tile = sorted_pool.tile([P, UNIT_BLOCKS * K], BF16, align_bytes=64)
+            sort_halves(tile[:], x_tiles[unit][:])
+            sorted_tiles[unit] = tile
+
+        def transpose_block(bank_part, words, blocks, b):
             for u in range(HALVES):
-                nc.tensor.transpose(bank_part[:, u, :], words[:, u : HALVES * P : HALVES], identity[:])
+                first = (u * blocks + b) * P
+                nc.tensor.transpose(bank_part[:, u, :], words[:, first : first + P], identity[:])
 
         def transpose_unit(unit):
-            words = x_tiles[unit][:].bitcast(F32)
+            words = sorted_tiles[unit][:].bitcast(F32)
             grouped = staged.tile([P, UNIT_BLOCKS * P * PACK], BF16, align_bytes=64)
             grouped_words = grouped[:].bitcast(F32)
             for h in range(UNIT_BANKS):
                 bank = flipped.tile([P, BANK_BLOCKS, HALVES, P], F32)
                 for a in range(BANK_BLOCKS):
-                    first = (h * BANK_BLOCKS + a) * HALVES * P
-                    transpose_block(bank[:, a], words[:, first : first + HALVES * P])
+                    transpose_block(bank[:, a], words, UNIT_BLOCKS, h * BANK_BLOCKS + a)
                 src = bank[:].rearrange("p a u j -> p a j u")
                 dst = grouped_words[:, h * BANK_WORDS : (h + 1) * BANK_WORDS].rearrange(
                     "p (a j u) -> p a j u", a=BANK_BLOCKS, u=HALVES
                 )
-                if (unit * UNIT_BANKS + h) % VECTOR_EVERY == VECTOR_EVERY - 1:
-                    nc.vector.tensor_copy(out=dst, in_=src)
-                else:
-                    nc.scalar.copy(out=dst, in_=src)
+                nc.scalar.copy(out=dst, in_=src)
             grouped_tiles[unit] = grouped
 
         def prepare_gate():
             bank = flipped.tile([P, BANK_BLOCKS, HALVES, P], F32)
-            transpose_block(bank[:, 0], gate[:].bitcast(F32))
+            transpose_block(bank[:, 0], gate_sorted[:].bitcast(F32), 1, 0)
             nc.vector.tensor_copy(
                 out=gate_grouped[:].bitcast(F32).rearrange("p (j u) -> p j u", u=HALVES),
                 in_=bank[:, 0].rearrange("p u j -> p j u"),
@@ -132,10 +144,7 @@ def tile_testmmrsmodel_t_kernel(tc, hidden_states, gate_proj, world_size, out):
         def store_strip(strip):
             result = out_pool.tile([P, UNIT_BLOCKS, WIDTH], F32)
             for b in range(UNIT_BLOCKS):
-                if b % 2 == 0:
-                    nc.scalar.copy(out=result[:, b, :], in_=sums[b][:])
-                else:
-                    nc.vector.tensor_copy(out=result[:, b, :], in_=sums[b][:])
+                nc.scalar.copy(out=result[:, b, :], in_=sums[b][:])
             first = strip * UNIT_BLOCKS * WIDTH
             nc.sync.dma_start(
                 out=out_dram[:, first : first + UNIT_BLOCKS * WIDTH],
@@ -145,16 +154,22 @@ def tile_testmmrsmodel_t_kernel(tc, hidden_states, gate_proj, world_size, out):
         def units_of(run):
             return range(run * RUN_UNITS, (run + 1) * RUN_UNITS)
 
+        loaded = 0
         nc.scalar.dma_start(out=gate[:], in_=gate_proj)
-        for unit in range(UNITS):
-            load(unit)
-        make_identity(nc, identity[:])
 
-        for t in range(RUNS + 2):
-            if 1 <= t <= RUNS:
-                for unit in units_of(t - 1):
-                    quantise_unit(unit)
-            if t < RUNS:
+        for t in range(-1, RUNS + 2):
+            while loaded < min(UNITS, max(0, t) * RUN_UNITS + LOADS_AHEAD):
+                load(loaded)
+                loaded += 1
+            if t == -1:
+                make_identity(nc, identity[:])
+                sort_halves(gate_sorted[:], gate[:])
+            for i in range(RUN_UNITS):
+                if 1 <= t <= RUNS:
+                    quantise_unit((t - 1) * RUN_UNITS + i)
+                if t + 1 < RUNS:
+                    sort_unit((t + 1) * RUN_UNITS + i)
+            if 0 <= t < RUNS:
                 for unit in units_of(t):
                     transpose_unit(unit)
             if t == 0:

@@ -17,20 +17,46 @@ CHUNKS = 8
 ROWS = 2048
 K = 512
 WIDTH = 128
+WORDS = K // 2
 
 RUN_WORDS = 8
 ROWS_PER_PARTITION = ROWS // P
-UNIT_BLOCKS = 4
-STRIPS = ROWS_PER_PARTITION // UNIT_BLOCKS
-UNITS = STRIPS * CHUNKS
+STRIP_BLOCKS = 4
+STRIPS = ROWS_PER_PARTITION // STRIP_BLOCKS
 BANK_BLOCKS = 2
-UNIT_BANKS = UNIT_BLOCKS // BANK_BLOCKS
-BANK_WORDS = BANK_BLOCKS * HALVES * P
-RUN_UNITS = 2
-RUNS = UNITS // RUN_UNITS
-LOADS_AHEAD = 14
+FREE_BANKS = 4
+RUN_CHUNKS = 2
+RUNS = STRIPS * CHUNKS // RUN_CHUNKS
+UNITS = STRIPS * CHUNKS
+STRIDED_EVERY = 4
+RUNS_AHEAD = 7
 
 FLOPS = 2 * CHUNKS * ROWS * K * WIDTH
+
+
+def pieces_of(run):
+    strip, pair = divmod(run, CHUNKS // RUN_CHUNKS)
+    first, second = pair * RUN_CHUNKS, pair * RUN_CHUNKS + 1
+    half = STRIP_BLOCKS // 2
+    if run == 0:
+        return [(strip, first, 0, half), (strip, first, half, half), (strip, second, 0, STRIP_BLOCKS)]
+    if run == RUNS - 1:
+        return [(strip, first, 0, STRIP_BLOCKS), (strip, second, 0, half), (strip, second, half, half)]
+    return [(strip, first, 0, STRIP_BLOCKS), (strip, second, 0, STRIP_BLOCKS)]
+
+
+def unit_of(piece):
+    return piece[0] * CHUNKS + piece[1]
+
+
+def is_sorted(piece):
+    unit = unit_of(piece)
+    return RUN_CHUNKS <= unit < (RUNS - 1) * RUN_CHUNKS and unit % STRIDED_EVERY != STRIDED_EVERY - 1
+
+
+def vector_empties(piece, first):
+    unit = unit_of(piece)
+    return (unit == 0 or unit == UNITS - 1) and piece[2] + first >= BANK_BLOCKS
 
 
 def tile_testmmrsmodel_t_kernel(tc, hidden_states, gate_proj, world_size, out):
@@ -44,33 +70,33 @@ def tile_testmmrsmodel_t_kernel(tc, hidden_states, gate_proj, world_size, out):
 
     with ExitStack() as stack:
         const = stack.enter_context(tc.tile_pool(name="const", bufs=1))
-        x_pool = stack.enter_context(tc.tile_pool(name="x", bufs=UNITS))
-        staged = stack.enter_context(tc.tile_pool(name="staged", bufs=3 * RUN_UNITS))
-        sorted_pool = stack.enter_context(tc.tile_pool(name="sorted", bufs=2 * RUN_UNITS))
-        out_pool = stack.enter_context(tc.tile_pool(name="result", bufs=STRIPS))
-        flipped = stack.enter_context(tc.psum_pool(name="flipped", bufs=RUN_UNITS * UNIT_BANKS))
+        x_pool = stack.enter_context(tc.tile_pool(name="x", bufs=2 * RUNS + 2))
+        sorted_pool = stack.enter_context(tc.tile_pool(name="sorted", bufs=4))
+        staged = stack.enter_context(tc.tile_pool(name="staged", bufs=7))
+        out_pool = stack.enter_context(tc.tile_pool(name="result", bufs=2 * STRIPS))
+        flipped = stack.enter_context(tc.psum_pool(name="flipped", bufs=FREE_BANKS))
         sums_pool = stack.enter_context(tc.psum_pool(name="sums", bufs=1))
         stack.enter_context(tc.manual_schedule())
 
         identity = const.tile([P, P], F32)
         gate = const.tile([P, K], BF16)
         gate_sorted = const.tile([P, K], BF16)
-        gate_grouped = const.tile([P, WIDTH * PACK], BF16, align_bytes=64)
-        gate_codes = const.tile([P, WIDTH], U32, align_bytes=64)
-        gate_scales = const.tile([P, WIDTH], U8, align_bytes=64)
+        gate_grouped = const.tile([P, 2 * WIDTH * PACK], BF16, align_bytes=64)
+        gate_codes = const.tile([P, 2 * WIDTH], U32, align_bytes=64)
+        gate_scales = const.tile([P, 2 * WIDTH], U8, align_bytes=64)
 
-        sorted_tiles = {}
         x_tiles = {}
+        sorted_tiles = {}
         grouped_tiles = {}
         mx_tiles = {}
         sums = {}
 
-        def load(unit):
-            strip, chunk = divmod(unit, CHUNKS)
-            x = x_pool.tile([P, UNIT_BLOCKS * K], BF16)
-            first = strip * UNIT_BLOCKS * K
-            nc.sync.dma_start(out=x[:], in_=x_dram[:, chunk, first : first + UNIT_BLOCKS * K])
-            x_tiles[unit] = x
+        def load(piece):
+            strip, chunk, first, blocks = piece
+            x = x_pool.tile([P, blocks * K], BF16)
+            start = (strip * STRIP_BLOCKS + first) * K
+            nc.sync.dma_start(out=x[:], in_=x_dram[:, chunk, start : start + blocks * K])
+            x_tiles[piece] = x
 
         def sort_halves(dst, src):
             nc.vector.tensor_copy(
@@ -78,102 +104,123 @@ def tile_testmmrsmodel_t_kernel(tc, hidden_states, gate_proj, world_size, out):
                 in_=src.rearrange("p (c u i) -> p u c i", u=HALVES, i=2 * RUN_WORDS),
             )
 
-        def sort_unit(unit):
-            tile = sorted_pool.tile([P, UNIT_BLOCKS * K], BF16, align_bytes=64)
-            sort_halves(tile[:], x_tiles[unit][:])
-            sorted_tiles[unit] = tile
+        def sort_piece(piece):
+            tile = sorted_pool.tile([P, piece[3] * K], BF16, align_bytes=64)
+            sort_halves(tile[:], x_tiles[piece][:])
+            sorted_tiles[piece] = tile
 
-        def transpose_block(bank_part, words, blocks, b):
+        def flip_sorted(bank_part, words, blocks, b):
             for u in range(HALVES):
                 first = (u * blocks + b) * P
                 nc.tensor.transpose(bank_part[:, u, :], words[:, first : first + P], identity[:])
 
-        def transpose_unit(unit):
-            words = sorted_tiles[unit][:].bitcast(F32)
-            grouped = staged.tile([P, UNIT_BLOCKS * P * PACK], BF16, align_bytes=64)
+        def flip_strided(bank_part, words, b):
+            for u in range(HALVES):
+                part = words[:, b * WORDS + u : (b + 1) * WORDS : HALVES]
+                nc.tensor.transpose(bank_part[:, u, :], part, identity[:])
+
+        def flip_piece(piece):
+            blocks = piece[3]
+            grouped = staged.tile([P, blocks * P * PACK], BF16, align_bytes=64)
             grouped_words = grouped[:].bitcast(F32)
-            for h in range(UNIT_BANKS):
+            for first in range(0, blocks, BANK_BLOCKS):
                 bank = flipped.tile([P, BANK_BLOCKS, HALVES, P], F32)
                 for a in range(BANK_BLOCKS):
-                    transpose_block(bank[:, a], words, UNIT_BLOCKS, h * BANK_BLOCKS + a)
+                    if is_sorted(piece):
+                        flip_sorted(bank[:, a], sorted_tiles[piece][:].bitcast(F32), blocks, first + a)
+                    else:
+                        flip_strided(bank[:, a], x_tiles[piece][:].bitcast(F32), first + a)
                 src = bank[:].rearrange("p a u j -> p a j u")
-                dst = grouped_words[:, h * BANK_WORDS : (h + 1) * BANK_WORDS].rearrange(
+                dst = grouped_words[:, first * WORDS : (first + BANK_BLOCKS) * WORDS].rearrange(
                     "p (a j u) -> p a j u", a=BANK_BLOCKS, u=HALVES
                 )
-                nc.scalar.copy(out=dst, in_=src)
-            grouped_tiles[unit] = grouped
+                if vector_empties(piece, first):
+                    nc.vector.tensor_copy(out=dst, in_=src)
+                else:
+                    nc.scalar.copy(out=dst, in_=src)
+            grouped_tiles[piece] = grouped
 
         def prepare_gate():
-            bank = flipped.tile([P, BANK_BLOCKS, HALVES, P], F32)
-            transpose_block(bank[:, 0], gate_sorted[:].bitcast(F32), 1, 0)
-            nc.vector.tensor_copy(
-                out=gate_grouped[:].bitcast(F32).rearrange("p (j u) -> p j u", u=HALVES),
-                in_=bank[:, 0].rearrange("p u j -> p j u"),
+            bank = flipped.tile([P, 2, HALVES, P], F32)
+            flip_strided(bank[:, 0], gate[:].bitcast(F32), 0)
+            flip_sorted(bank[:, 1], gate_sorted[:].bitcast(F32), 1, 0)
+            nc.scalar.copy(
+                out=gate_grouped[:].bitcast(F32).rearrange("p (a j u) -> p a j u", a=2, u=HALVES),
+                in_=bank[:].rearrange("p a u j -> p a j u"),
             )
+
+        def quantise_gate():
             nc.vector.quantize_mx(
                 out=gate_codes[:].bitcast(FP8X4), scales=gate_scales[:], in_=gate_grouped[:]
             )
 
-        def quantise_unit(unit):
-            codes = staged.tile([P, UNIT_BLOCKS * P], U32, align_bytes=64)
-            scales = staged.tile([P, UNIT_BLOCKS * P], U8, align_bytes=64)
+        def quantise_piece(piece):
+            codes = staged.tile([P, piece[3] * P], U32, align_bytes=64)
+            scales = staged.tile([P, piece[3] * P], U8, align_bytes=64)
             nc.vector.quantize_mx(
-                out=codes[:].bitcast(FP8X4), scales=scales[:], in_=grouped_tiles[unit][:]
+                out=codes[:].bitcast(FP8X4), scales=scales[:], in_=grouped_tiles[piece][:]
             )
-            mx_tiles[unit] = (codes, scales)
+            mx_tiles[piece] = (codes, scales)
 
-        def multiply_unit(unit):
-            strip, chunk = divmod(unit, CHUNKS)
-            codes, scales = mx_tiles[unit]
-            for b in range(UNIT_BLOCKS):
+        def multiply_piece(piece):
+            strip, chunk, first, blocks = piece
+            codes, scales = mx_tiles[piece]
+            gate_cols = slice(WIDTH, 2 * WIDTH) if is_sorted(piece) else slice(0, WIDTH)
+            for a in range(blocks):
+                b = first + a
                 if chunk == 0:
                     sums[b] = sums_pool.tile([P, WIDTH], F32, name="sum%d" % b)
-                rows = slice(b * P, (b + 1) * P)
+                rows = slice(a * P, (a + 1) * P)
                 nc.tensor.matmul_mx(
                     out=sums[b][:],
                     lhsT=codes[:, rows].bitcast(FP8X4),
                     lhsT_scale=scales[:, rows],
-                    rhs=gate_codes[:].bitcast(FP8X4),
-                    rhs_scale=gate_scales[:],
+                    rhs=gate_codes[:, gate_cols].bitcast(FP8X4),
+                    rhs_scale=gate_scales[:, gate_cols],
                     start=(chunk == 0),
                     stop=(chunk == CHUNKS - 1),
                 )
             if chunk == CHUNKS - 1:
-                store_strip(strip)
+                store(strip, first, blocks)
 
-        def store_strip(strip):
-            result = out_pool.tile([P, UNIT_BLOCKS, WIDTH], F32)
-            for b in range(UNIT_BLOCKS):
-                nc.scalar.copy(out=result[:, b, :], in_=sums[b][:])
-            first = strip * UNIT_BLOCKS * WIDTH
+        def store(strip, first, blocks):
+            result = out_pool.tile([P, blocks, WIDTH], F32)
+            for a in range(blocks):
+                if a % 2 == 0:
+                    nc.scalar.copy(out=result[:, a, :], in_=sums[first + a][:])
+                else:
+                    nc.vector.tensor_copy(out=result[:, a, :], in_=sums[first + a][:])
+            start = (strip * STRIP_BLOCKS + first) * WIDTH
             nc.sync.dma_start(
-                out=out_dram[:, first : first + UNIT_BLOCKS * WIDTH],
+                out=out_dram[:, start : start + blocks * WIDTH],
                 in_=result[:].rearrange("p b o -> p (b o)"),
             )
 
-        def units_of(run):
-            return range(run * RUN_UNITS, (run + 1) * RUN_UNITS)
-
+        nc.sync.dma_start(out=gate[:], in_=gate_proj)
         loaded = 0
-        nc.scalar.dma_start(out=gate[:], in_=gate_proj)
-
         for t in range(-1, RUNS + 2):
-            while loaded < min(UNITS, max(0, t) * RUN_UNITS + LOADS_AHEAD):
-                load(loaded)
+            while loaded < min(RUNS, max(0, t) + RUNS_AHEAD):
+                for piece in pieces_of(loaded):
+                    load(piece)
                 loaded += 1
             if t == -1:
                 make_identity(nc, identity[:])
                 sort_halves(gate_sorted[:], gate[:])
-            for i in range(RUN_UNITS):
-                if 1 <= t <= RUNS:
-                    quantise_unit((t - 1) * RUN_UNITS + i)
-                if t + 1 < RUNS:
-                    sort_unit((t + 1) * RUN_UNITS + i)
-            if 0 <= t < RUNS:
-                for unit in units_of(t):
-                    transpose_unit(unit)
-            if t == 0:
                 prepare_gate()
+            if t == 0:
+                quantise_gate()
+                for piece in pieces_of(t):
+                    flip_piece(piece)
+            behind = pieces_of(t - 1) if 1 <= t <= RUNS else []
+            ahead = [p for p in pieces_of(t + 1) if is_sorted(p)] if t + 1 < RUNS else []
+            for i in range(max(len(behind), len(ahead))):
+                if i < len(behind):
+                    quantise_piece(behind[i])
+                if i < len(ahead):
+                    sort_piece(ahead[i])
+            if 1 <= t < RUNS:
+                for piece in pieces_of(t):
+                    flip_piece(piece)
             if t >= 2:
-                for unit in units_of(t - 2):
-                    multiply_unit(unit)
+                for piece in pieces_of(t - 2):
+                    multiply_piece(piece)

@@ -27,8 +27,6 @@ BANK_BLOCKS = 2
 FREE_BANKS = 4
 RUN_CHUNKS = 2
 RUNS = STRIPS * CHUNKS // RUN_CHUNKS
-UNITS = STRIPS * CHUNKS
-STRIDED_EVERY = 4
 RUNS_AHEAD = 7
 
 FLOPS = 2 * CHUNKS * ROWS * K * WIDTH
@@ -45,20 +43,6 @@ def pieces_of(run):
     return [(strip, first, 0, STRIP_BLOCKS), (strip, second, 0, STRIP_BLOCKS)]
 
 
-def unit_of(piece):
-    return piece[0] * CHUNKS + piece[1]
-
-
-def is_sorted(piece):
-    unit = unit_of(piece)
-    return RUN_CHUNKS <= unit < (RUNS - 1) * RUN_CHUNKS and unit % STRIDED_EVERY != STRIDED_EVERY - 1
-
-
-def vector_empties(piece, first):
-    unit = unit_of(piece)
-    return (unit == 0 or unit == UNITS - 1) and piece[2] + first >= BANK_BLOCKS
-
-
 def tile_testmmrsmodel_t_kernel(tc, hidden_states, gate_proj, world_size, out):
     nc = tc.nc
     assert world_size == CHUNKS
@@ -71,7 +55,7 @@ def tile_testmmrsmodel_t_kernel(tc, hidden_states, gate_proj, world_size, out):
     with ExitStack() as stack:
         const = stack.enter_context(tc.tile_pool(name="const", bufs=1))
         x_pool = stack.enter_context(tc.tile_pool(name="x", bufs=2 * RUNS + 2))
-        sorted_pool = stack.enter_context(tc.tile_pool(name="sorted", bufs=4))
+        sorted_pool = stack.enter_context(tc.tile_pool(name="sorted", bufs=5))
         staged = stack.enter_context(tc.tile_pool(name="staged", bufs=7))
         out_pool = stack.enter_context(tc.tile_pool(name="result", bufs=2 * STRIPS))
         flipped = stack.enter_context(tc.psum_pool(name="flipped", bufs=FREE_BANKS))
@@ -81,9 +65,9 @@ def tile_testmmrsmodel_t_kernel(tc, hidden_states, gate_proj, world_size, out):
         identity = const.tile([P, P], F32)
         gate = const.tile([P, K], BF16)
         gate_sorted = const.tile([P, K], BF16)
-        gate_grouped = const.tile([P, 2 * WIDTH * PACK], BF16, align_bytes=64)
-        gate_codes = const.tile([P, 2 * WIDTH], U32, align_bytes=64)
-        gate_scales = const.tile([P, 2 * WIDTH], U8, align_bytes=64)
+        gate_grouped = const.tile([P, WIDTH * PACK], BF16, align_bytes=64)
+        gate_codes = const.tile([P, WIDTH], U32, align_bytes=64)
+        gate_scales = const.tile([P, WIDTH], U8, align_bytes=64)
 
         x_tiles = {}
         sorted_tiles = {}
@@ -114,11 +98,6 @@ def tile_testmmrsmodel_t_kernel(tc, hidden_states, gate_proj, world_size, out):
                 first = (u * blocks + b) * P
                 nc.tensor.transpose(bank_part[:, u, :], words[:, first : first + P], identity[:])
 
-        def flip_strided(bank_part, words, b):
-            for u in range(HALVES):
-                part = words[:, b * WORDS + u : (b + 1) * WORDS : HALVES]
-                nc.tensor.transpose(bank_part[:, u, :], part, identity[:])
-
         def flip_piece(piece):
             blocks = piece[3]
             grouped = staged.tile([P, blocks * P * PACK], BF16, align_bytes=64)
@@ -126,27 +105,20 @@ def tile_testmmrsmodel_t_kernel(tc, hidden_states, gate_proj, world_size, out):
             for first in range(0, blocks, BANK_BLOCKS):
                 bank = flipped.tile([P, BANK_BLOCKS, HALVES, P], F32)
                 for a in range(BANK_BLOCKS):
-                    if is_sorted(piece):
-                        flip_sorted(bank[:, a], sorted_tiles[piece][:].bitcast(F32), blocks, first + a)
-                    else:
-                        flip_strided(bank[:, a], x_tiles[piece][:].bitcast(F32), first + a)
+                    flip_sorted(bank[:, a], sorted_tiles[piece][:].bitcast(F32), blocks, first + a)
                 src = bank[:].rearrange("p a u j -> p a j u")
                 dst = grouped_words[:, first * WORDS : (first + BANK_BLOCKS) * WORDS].rearrange(
                     "p (a j u) -> p a j u", a=BANK_BLOCKS, u=HALVES
                 )
-                if vector_empties(piece, first):
-                    nc.vector.tensor_copy(out=dst, in_=src)
-                else:
-                    nc.scalar.copy(out=dst, in_=src)
+                nc.scalar.copy(out=dst, in_=src)
             grouped_tiles[piece] = grouped
 
         def prepare_gate():
-            bank = flipped.tile([P, 2, HALVES, P], F32)
-            flip_strided(bank[:, 0], gate[:].bitcast(F32), 0)
-            flip_sorted(bank[:, 1], gate_sorted[:].bitcast(F32), 1, 0)
+            bank = flipped.tile([P, BANK_BLOCKS, HALVES, P], F32)
+            flip_sorted(bank[:, 0], gate_sorted[:].bitcast(F32), 1, 0)
             nc.scalar.copy(
-                out=gate_grouped[:].bitcast(F32).rearrange("p (a j u) -> p a j u", a=2, u=HALVES),
-                in_=bank[:].rearrange("p a u j -> p a j u"),
+                out=gate_grouped[:].bitcast(F32).rearrange("p (j u) -> p j u", u=HALVES),
+                in_=bank[:, 0].rearrange("p u j -> p j u"),
             )
 
         def quantise_gate():
@@ -165,7 +137,6 @@ def tile_testmmrsmodel_t_kernel(tc, hidden_states, gate_proj, world_size, out):
         def multiply_piece(piece):
             strip, chunk, first, blocks = piece
             codes, scales = mx_tiles[piece]
-            gate_cols = slice(WIDTH, 2 * WIDTH) if is_sorted(piece) else slice(0, WIDTH)
             for a in range(blocks):
                 b = first + a
                 if chunk == 0:
@@ -175,8 +146,8 @@ def tile_testmmrsmodel_t_kernel(tc, hidden_states, gate_proj, world_size, out):
                     out=sums[b][:],
                     lhsT=codes[:, rows].bitcast(FP8X4),
                     lhsT_scale=scales[:, rows],
-                    rhs=gate_codes[:, gate_cols].bitcast(FP8X4),
-                    rhs_scale=gate_scales[:, gate_cols],
+                    rhs=gate_codes[:].bitcast(FP8X4),
+                    rhs_scale=gate_scales[:],
                     start=(chunk == 0),
                     stop=(chunk == CHUNKS - 1),
                 )
@@ -207,18 +178,16 @@ def tile_testmmrsmodel_t_kernel(tc, hidden_states, gate_proj, world_size, out):
                 make_identity(nc, identity[:])
                 sort_halves(gate_sorted[:], gate[:])
                 prepare_gate()
-            if t == 0:
-                quantise_gate()
-                for piece in pieces_of(t):
-                    flip_piece(piece)
             behind = pieces_of(t - 1) if 1 <= t <= RUNS else []
-            ahead = [p for p in pieces_of(t + 1) if is_sorted(p)] if t + 1 < RUNS else []
+            ahead = pieces_of(t + 1) if t + 1 < RUNS else []
             for i in range(max(len(behind), len(ahead))):
                 if i < len(behind):
                     quantise_piece(behind[i])
                 if i < len(ahead):
                     sort_piece(ahead[i])
-            if 1 <= t < RUNS:
+            if t == 0:
+                quantise_gate()
+            if 0 <= t < RUNS:
                 for piece in pieces_of(t):
                     flip_piece(piece)
             if t >= 2:

@@ -19,7 +19,8 @@ K = 512
 WIDTH = 128
 WORDS = K // 2
 
-RUN_WORDS = 8
+RUN_K = 16
+PAIRS = 8
 ROWS_PER_PARTITION = ROWS // P
 STRIP_BLOCKS = 4
 STRIPS = ROWS_PER_PARTITION // STRIP_BLOCKS
@@ -55,7 +56,7 @@ def tile_testmmrsmodel_t_kernel(tc, hidden_states, gate_proj, world_size, out):
     with ExitStack() as stack:
         const = stack.enter_context(tc.tile_pool(name="const", bufs=1))
         x_pool = stack.enter_context(tc.tile_pool(name="x", bufs=2 * RUNS + 2))
-        sorted_pool = stack.enter_context(tc.tile_pool(name="sorted", bufs=5))
+        partner_pool = stack.enter_context(tc.tile_pool(name="partners", bufs=5))
         staged = stack.enter_context(tc.tile_pool(name="staged", bufs=7))
         out_pool = stack.enter_context(tc.tile_pool(name="result", bufs=2 * STRIPS))
         flipped = stack.enter_context(tc.psum_pool(name="flipped", bufs=FREE_BANKS))
@@ -64,13 +65,13 @@ def tile_testmmrsmodel_t_kernel(tc, hidden_states, gate_proj, world_size, out):
 
         identity = const.tile([P, P], F32)
         gate = const.tile([P, K], BF16)
-        gate_sorted = const.tile([P, K], BF16)
+        gate_partners = const.tile([P, K // 2], BF16)
         gate_grouped = const.tile([P, WIDTH * PACK], BF16, align_bytes=64)
         gate_codes = const.tile([P, WIDTH], U32, align_bytes=64)
         gate_scales = const.tile([P, WIDTH], U8, align_bytes=64)
 
         x_tiles = {}
-        sorted_tiles = {}
+        partner_tiles = {}
         grouped_tiles = {}
         mx_tiles = {}
         sums = {}
@@ -82,21 +83,26 @@ def tile_testmmrsmodel_t_kernel(tc, hidden_states, gate_proj, world_size, out):
             nc.sync.dma_start(out=x[:], in_=x_dram[:, chunk, start : start + blocks * K])
             x_tiles[piece] = x
 
-        def sort_halves(dst, src):
-            nc.vector.tensor_copy(
-                out=dst.rearrange("p (u c i) -> p u c i", u=HALVES, i=2 * RUN_WORDS),
-                in_=src.rearrange("p (c u i) -> p u c i", u=HALVES, i=2 * RUN_WORDS),
+        def runs_of(rows):
+            return rows.rearrange(
+                "p (b h m o i) -> p b h m o i", h=HALVES, m=PAIRS, o=2, i=RUN_K
             )
 
-        def sort_piece(piece):
-            tile = sorted_pool.tile([P, piece[3] * K], BF16, align_bytes=64)
-            sort_halves(tile[:], x_tiles[piece][:])
-            sorted_tiles[piece] = tile
+        def copy_partners(partners, rows):
+            nc.vector.tensor_copy(
+                out=partners.rearrange("p (b m h i) -> p b m h i", m=PAIRS, h=HALVES, i=RUN_K),
+                in_=runs_of(rows)[:, :, :, :, 1, :].rearrange("p b h m i -> p b m h i"),
+            )
 
-        def flip_sorted(bank_part, words, blocks, b):
-            for u in range(HALVES):
-                first = (u * blocks + b) * P
-                nc.tensor.transpose(bank_part[:, u, :], words[:, first : first + P], identity[:])
+        def gather_firsts(rows):
+            runs = runs_of(rows)
+            nc.vector.tensor_copy(out=runs[:, :, 0, :, 1, :], in_=runs[:, :, 1, :, 0, :])
+
+        def flip_block(bank_part, rows, partners, b):
+            firsts = rows.bitcast(F32)[:, b * WORDS : b * WORDS + P]
+            seconds = partners.bitcast(F32)[:, b * P : (b + 1) * P]
+            nc.tensor.transpose(bank_part[:, 0, :], firsts, identity[:])
+            nc.tensor.transpose(bank_part[:, 1, :], seconds, identity[:])
 
         def flip_piece(piece):
             blocks = piece[3]
@@ -105,7 +111,7 @@ def tile_testmmrsmodel_t_kernel(tc, hidden_states, gate_proj, world_size, out):
             for first in range(0, blocks, BANK_BLOCKS):
                 bank = flipped.tile([P, BANK_BLOCKS, HALVES, P], F32)
                 for a in range(BANK_BLOCKS):
-                    flip_sorted(bank[:, a], sorted_tiles[piece][:].bitcast(F32), blocks, first + a)
+                    flip_block(bank[:, a], x_tiles[piece][:], partner_tiles[piece][:], first + a)
                 src = bank[:].rearrange("p a u j -> p a j u")
                 dst = grouped_words[:, first * WORDS : (first + BANK_BLOCKS) * WORDS].rearrange(
                     "p (a j u) -> p a j u", a=BANK_BLOCKS, u=HALVES
@@ -115,7 +121,7 @@ def tile_testmmrsmodel_t_kernel(tc, hidden_states, gate_proj, world_size, out):
 
         def prepare_gate():
             bank = flipped.tile([P, BANK_BLOCKS, HALVES, P], F32)
-            flip_sorted(bank[:, 0], gate_sorted[:].bitcast(F32), 1, 0)
+            flip_block(bank[:, 0], gate[:], gate_partners[:], 0)
             nc.scalar.copy(
                 out=gate_grouped[:].bitcast(F32).rearrange("p (j u) -> p j u", u=HALVES),
                 in_=bank[:, 0].rearrange("p u j -> p j u"),
@@ -176,15 +182,20 @@ def tile_testmmrsmodel_t_kernel(tc, hidden_states, gate_proj, world_size, out):
                 loaded += 1
             if t == -1:
                 make_identity(nc, identity[:])
-                sort_halves(gate_sorted[:], gate[:])
+                copy_partners(gate_partners[:], gate[:])
+                gather_firsts(gate[:])
                 prepare_gate()
             behind = pieces_of(t - 1) if 1 <= t <= RUNS else []
             ahead = pieces_of(t + 1) if t + 1 < RUNS else []
             for i in range(max(len(behind), len(ahead))):
+                if i < len(ahead):
+                    partners = partner_pool.tile([P, ahead[i][3] * K // 2], BF16, align_bytes=64)
+                    partner_tiles[ahead[i]] = partners
+                    copy_partners(partners[:], x_tiles[ahead[i]][:])
                 if i < len(behind):
                     quantise_piece(behind[i])
                 if i < len(ahead):
-                    sort_piece(ahead[i])
+                    gather_firsts(x_tiles[ahead[i]][:])
             if t == 0:
                 quantise_gate()
             if 0 <= t < RUNS:

@@ -26,22 +26,27 @@ STRIP_BLOCKS = 4
 STRIPS = ROWS_PER_PARTITION // STRIP_BLOCKS
 BANK_BLOCKS = 2
 FREE_BANKS = 4
-RUN_CHUNKS = 2
-RUNS = STRIPS * CHUNKS // RUN_CHUNKS
-RUNS_AHEAD = 7
+RUN_UNITS = 2
+UNITS = STRIPS * CHUNKS
+HEAD_UNITS = 2
 
 FLOPS = 2 * CHUNKS * ROWS * K * WIDTH
 
 
-def pieces_of(run):
-    strip, pair = divmod(run, CHUNKS // RUN_CHUNKS)
-    first, second = pair * RUN_CHUNKS, pair * RUN_CHUNKS + 1
+def pieces_of(unit):
+    strip, chunk = divmod(unit, CHUNKS)
     half = STRIP_BLOCKS // 2
-    if run == 0:
-        return [(strip, first, 0, half), (strip, first, half, half), (strip, second, 0, STRIP_BLOCKS)]
-    if run == RUNS - 1:
-        return [(strip, first, 0, STRIP_BLOCKS), (strip, second, 0, half), (strip, second, half, half)]
-    return [(strip, first, 0, STRIP_BLOCKS), (strip, second, 0, STRIP_BLOCKS)]
+    if unit in (0, UNITS - 1):
+        return [(strip, chunk, 0, half), (strip, chunk, half, half)]
+    return [(strip, chunk, 0, STRIP_BLOCKS)]
+
+
+def make_runs():
+    starts = list(range(HEAD_UNITS)) + list(range(HEAD_UNITS, UNITS, RUN_UNITS)) + [UNITS]
+    return [
+        [piece for unit in range(a, b) for piece in pieces_of(unit)]
+        for a, b in zip(starts[:-1], starts[1:])
+    ]
 
 
 def tile_testmmrsmodel_t_kernel(tc, hidden_states, gate_proj, world_size, out):
@@ -53,9 +58,10 @@ def tile_testmmrsmodel_t_kernel(tc, hidden_states, gate_proj, world_size, out):
     x_dram = hidden_states.rearrange("r (p i) k -> p r (i k)", i=ROWS_PER_PARTITION)
     out_dram = out.rearrange("(p i) o -> p (i o)", i=ROWS_PER_PARTITION)
 
+    runs = make_runs()
     with ExitStack() as stack:
         const = stack.enter_context(tc.tile_pool(name="const", bufs=1))
-        x_pool = stack.enter_context(tc.tile_pool(name="x", bufs=2 * RUNS + 2))
+        x_pool = stack.enter_context(tc.tile_pool(name="x", bufs=UNITS + 2))
         partner_pool = stack.enter_context(tc.tile_pool(name="partners", bufs=5))
         staged = stack.enter_context(tc.tile_pool(name="staged", bufs=7))
         out_pool = stack.enter_context(tc.tile_pool(name="result", bufs=2 * STRIPS))
@@ -174,19 +180,17 @@ def tile_testmmrsmodel_t_kernel(tc, hidden_states, gate_proj, world_size, out):
             )
 
         nc.sync.dma_start(out=gate[:], in_=gate_proj)
-        loaded = 0
-        for t in range(-1, RUNS + 2):
-            while loaded < min(RUNS, max(0, t) + RUNS_AHEAD):
-                for piece in pieces_of(loaded):
-                    load(piece)
-                loaded += 1
+        for pieces in runs:
+            for piece in pieces:
+                load(piece)
+        for t in range(-1, len(runs) + 2):
             if t == -1:
                 make_identity(nc, identity[:])
                 copy_partners(gate_partners[:], gate[:])
                 gather_firsts(gate[:])
                 prepare_gate()
-            behind = pieces_of(t - 1) if 1 <= t <= RUNS else []
-            ahead = pieces_of(t + 1) if t + 1 < RUNS else []
+            behind = runs[t - 1] if 1 <= t <= len(runs) else []
+            ahead = runs[t + 1] if t + 1 < len(runs) else []
             for i in range(max(len(behind), len(ahead))):
                 if i < len(ahead):
                     partners = partner_pool.tile([P, ahead[i][3] * K // 2], BF16, align_bytes=64)
@@ -198,9 +202,9 @@ def tile_testmmrsmodel_t_kernel(tc, hidden_states, gate_proj, world_size, out):
                     gather_firsts(x_tiles[ahead[i]][:])
             if t == 0:
                 quantise_gate()
-            if 0 <= t < RUNS:
-                for piece in pieces_of(t):
+            if 0 <= t < len(runs):
+                for piece in runs[t]:
                     flip_piece(piece)
             if t >= 2:
-                for piece in pieces_of(t - 2):
+                for piece in runs[t - 2]:
                     multiply_piece(piece)

from contextlib import ExitStack

import concourse.mybir as mybir
from concourse.masks import make_identity

F32 = mybir.dt.float32
BF16 = mybir.dt.bfloat16
U32 = mybir.dt.uint32
U8 = mybir.dt.uint8
FP8X4 = mybir.dt.float8_e4m3fn_x4

P = 128
PACK = 4
HALVES = 2

CHUNKS = 8
ROWS = 2048
K = 512
WIDTH = 128
WORDS = K // 2

RUN_K = 16
PAIRS = 8
ROWS_PER_PARTITION = ROWS // P
STRIP_BLOCKS = 4
STRIPS = ROWS_PER_PARTITION // STRIP_BLOCKS
BANK_BLOCKS = 2
FREE_BANKS = 4
RUN_UNITS = 2
UNITS = STRIPS * CHUNKS
HEAD_UNITS = 2

FLOPS = 2 * CHUNKS * ROWS * K * WIDTH


def pieces_of(unit):
    strip, chunk = divmod(unit, CHUNKS)
    half = STRIP_BLOCKS // 2
    if unit in (0, UNITS - 1):
        return [(strip, chunk, 0, half), (strip, chunk, half, half)]
    return [(strip, chunk, 0, STRIP_BLOCKS)]


def make_runs():
    starts = list(range(HEAD_UNITS)) + list(range(HEAD_UNITS, UNITS, RUN_UNITS)) + [UNITS]
    return [
        [piece for unit in range(a, b) for piece in pieces_of(unit)]
        for a, b in zip(starts[:-1], starts[1:])
    ]


def tile_testmmrsmodel_t_kernel(tc, hidden_states, gate_proj, world_size, out):
    nc = tc.nc
    assert world_size == CHUNKS
    assert tuple(hidden_states.shape) == (CHUNKS, ROWS, K)
    assert tuple(gate_proj.shape) == (WIDTH, K)

    x_dram = hidden_states.rearrange("r (p i) k -> p r (i k)", i=ROWS_PER_PARTITION)
    out_dram = out.rearrange("(p i) o -> p (i o)", i=ROWS_PER_PARTITION)

    runs = make_runs()
    with ExitStack() as stack:
        const = stack.enter_context(tc.tile_pool(name="const", bufs=1))
        x_pool = stack.enter_context(tc.tile_pool(name="x", bufs=UNITS + 2))
        partner_pool = stack.enter_context(tc.tile_pool(name="partners", bufs=5))
        staged = stack.enter_context(tc.tile_pool(name="staged", bufs=7))
        out_pool = stack.enter_context(tc.tile_pool(name="result", bufs=2 * STRIPS))
        flipped = stack.enter_context(tc.psum_pool(name="flipped", bufs=FREE_BANKS))
        sums_pool = stack.enter_context(tc.psum_pool(name="sums", bufs=1))
        stack.enter_context(tc.manual_schedule())

        identity = const.tile([P, P], F32)
        gate = const.tile([P, K], BF16)
        gate_partners = const.tile([P, K // 2], BF16)
        gate_grouped = const.tile([P, WIDTH * PACK], BF16, align_bytes=64)
        gate_codes = const.tile([P, WIDTH], U32, align_bytes=64)
        gate_scales = const.tile([P, WIDTH], U8, align_bytes=64)

        x_tiles = {}
        partner_tiles = {}
        grouped_tiles = {}
        mx_tiles = {}
        sums = {}

        def load(piece):
            strip, chunk, first, blocks = piece
            x = x_pool.tile([P, blocks * K], BF16)
            start = (strip * STRIP_BLOCKS + first) * K
            nc.sync.dma_start(out=x[:], in_=x_dram[:, chunk, start : start + blocks * K])
            x_tiles[piece] = x

        def runs_of(rows):
            return rows.rearrange(
                "p (b h m o i) -> p b h m o i", h=HALVES, m=PAIRS, o=2, i=RUN_K
            )

        def copy_partners(partners, rows):
            nc.vector.tensor_copy(
                out=partners.rearrange("p (b m h i) -> p b m h i", m=PAIRS, h=HALVES, i=RUN_K),
                in_=runs_of(rows)[:, :, :, :, 1, :].rearrange("p b h m i -> p b m h i"),
            )

        def gather_firsts(rows):
            runs = runs_of(rows)
            nc.vector.tensor_copy(out=runs[:, :, 0, :, 1, :], in_=runs[:, :, 1, :, 0, :])

        def flip_block(bank_part, rows, partners, b):
            firsts = rows.bitcast(F32)[:, b * WORDS : b * WORDS + P]
            seconds = partners.bitcast(F32)[:, b * P : (b + 1) * P]
            nc.tensor.transpose(bank_part[:, 0, :], firsts, identity[:])
            nc.tensor.transpose(bank_part[:, 1, :], seconds, identity[:])

        def flip_piece(piece):
            blocks = piece[3]
            grouped = staged.tile([P, blocks * P * PACK], BF16, align_bytes=64)
            grouped_words = grouped[:].bitcast(F32)
            for first in range(0, blocks, BANK_BLOCKS):
                bank = flipped.tile([P, BANK_BLOCKS, HALVES, P], F32)
                for a in range(BANK_BLOCKS):
                    flip_block(bank[:, a], x_tiles[piece][:], partner_tiles[piece][:], first + a)
                src = bank[:].rearrange("p a u j -> p a j u")
                dst = grouped_words[:, first * WORDS : (first + BANK_BLOCKS) * WORDS].rearrange(
                    "p (a j u) -> p a j u", a=BANK_BLOCKS, u=HALVES
                )
                nc.scalar.copy(out=dst, in_=src)
            grouped_tiles[piece] = grouped

        def prepare_gate():
            bank = flipped.tile([P, BANK_BLOCKS, HALVES, P], F32)
            flip_block(bank[:, 0], gate[:], gate_partners[:], 0)
            nc.scalar.copy(
                out=gate_grouped[:].bitcast(F32).rearrange("p (j u) -> p j u", u=HALVES),
                in_=bank[:, 0].rearrange("p u j -> p j u"),
            )

        def quantise_gate():
            nc.vector.quantize_mx(
                out=gate_codes[:].bitcast(FP8X4), scales=gate_scales[:], in_=gate_grouped[:]
            )

        def quantise_piece(piece):
            codes = staged.tile([P, piece[3] * P], U32, align_bytes=64)
            scales = staged.tile([P, piece[3] * P], U8, align_bytes=64)
            nc.vector.quantize_mx(
                out=codes[:].bitcast(FP8X4), scales=scales[:], in_=grouped_tiles[piece][:]
            )
            mx_tiles[piece] = (codes, scales)

        def multiply_piece(piece):
            strip, chunk, first, blocks = piece
            codes, scales = mx_tiles[piece]
            for a in range(blocks):
                b = first + a
                if chunk == 0:
                    sums[b] = sums_pool.tile([P, WIDTH], F32, name="sum%d" % b)
                rows = slice(a * P, (a + 1) * P)
                nc.tensor.matmul_mx(
                    out=sums[b][:],
                    lhsT=codes[:, rows].bitcast(FP8X4),
                    lhsT_scale=scales[:, rows],
                    rhs=gate_codes[:].bitcast(FP8X4),
                    rhs_scale=gate_scales[:],
                    start=(chunk == 0),
                    stop=(chunk == CHUNKS - 1),
                )
            if chunk == CHUNKS - 1:
                store(strip, first, blocks)

        def store(strip, first, blocks):
            result = out_pool.tile([P, blocks, WIDTH], F32)
            for a in range(blocks):
                if a % 2 == 0:
                    nc.scalar.copy(out=result[:, a, :], in_=sums[first + a][:])
                else:
                    nc.vector.tensor_copy(out=result[:, a, :], in_=sums[first + a][:])
            start = (strip * STRIP_BLOCKS + first) * WIDTH
            nc.sync.dma_start(
                out=out_dram[:, start : start + blocks * WIDTH],
                in_=result[:].rearrange("p b o -> p (b o)"),
            )

        nc.sync.dma_start(out=gate[:], in_=gate_proj)
        for pieces in runs:
            for piece in pieces:
                load(piece)
        for t in range(-1, len(runs) + 2):
            if t == -1:
                make_identity(nc, identity[:])
                copy_partners(gate_partners[:], gate[:])
                gather_firsts(gate[:])
                prepare_gate()
            behind = runs[t - 1] if 1 <= t <= len(runs) else []
            ahead = runs[t + 1] if t + 1 < len(runs) else []
            for i in range(max(len(behind), len(ahead))):
                if i < len(ahead):
                    partners = partner_pool.tile([P, ahead[i][3] * K // 2], BF16, align_bytes=64)
                    partner_tiles[ahead[i]] = partners
                    copy_partners(partners[:], x_tiles[ahead[i]][:])
                if i < len(behind):
                    quantise_piece(behind[i])
                if i < len(ahead):
                    gather_firsts(x_tiles[ahead[i]][:])
            if t == 0:
                quantise_gate()
            if 0 <= t < len(runs):
                for piece in runs[t]:
                    flip_piece(piece)
            if t >= 2:
                for piece in runs[t - 2]:
                    multiply_piece(piece)
